import numpy as np
import ml_dtypes


def mxq(x, axis, fmt="e4m3"):
    dtype, down = {"e4m3": (ml_dtypes.float8_e4m3fn, 7), "e5m2": (ml_dtypes.float8_e5m2, 14)}[fmt]
    v = np.moveaxis(np.asarray(x, np.float32).astype(ml_dtypes.bfloat16).astype(np.float64), axis, -1)
    blocks = v.reshape(v.shape[:-1] + (-1, 32))
    amax = np.abs(blocks).max(-1, keepdims=True)
    byte = np.maximum(np.where(amax > 0, np.frexp(amax)[1] - 1 + 127, 0) - down, 1)
    scale = np.exp2(byte - 127.0)
    codes = (blocks / scale).astype(np.float32).astype(dtype).astype(np.float64)
    return np.moveaxis((codes * scale).reshape(v.shape), -1, axis)


WIDE = False


def mx_kscale(k):
    if not WIDE:
        return np.ones(k)
    levels = np.array([10, -10, 5, -5, 0])
    a = np.random.permutation(np.resize(levels, k // 512 * 4)).reshape(k // 512, 4)
    idx = np.arange(k)
    return np.exp2(a[idx // 512, idx % 128 // 32])


BF16 = ml_dtypes.bfloat16


def bf(x):
    return np.asarray(x, np.float32).astype(BF16)


def f64(x):
    return np.asarray(x).astype(np.float64)


B, DIM, D2, T = 1, 512, 1024, 512


def setup_inputs():
    s, t = mx_kscale(D2), mx_kscale(T)
    es = 0.25 * s[None, :, None] * t[None, None, :]
    ss = 0.044 * np.sqrt(D2) / t[None, :, None]
    ps = 2.0 / np.sqrt(D2) / s[None, :]
    return {"E_re": bf(np.random.standard_normal((B, D2, T)) * es),
            "E_im": bf(np.random.standard_normal((B, D2, T)) * es),
            "S_re": bf(np.random.standard_normal((B, T, T)) * ss),
            "S_im": bf(np.random.standard_normal((B, T, T)) * ss),
            "WPV_re": bf(np.random.standard_normal((DIM, D2)) * ps),
            "WPV_im": bf(np.random.standard_normal((DIM, D2)) * ps)}


def reference(E_re, E_im, S_re, S_im, WPV_re, WPV_im):
    causal = np.triu(np.ones((T, T), dtype=bool))
    sr = mxq(np.where(causal, f64(S_re), 0.0), 1, "e4m3")
    si = mxq(np.where(causal, f64(S_im), 0.0), 1, "e4m3")
    er = mxq(f64(E_re), 2, "e4m3")
    ei = mxq(f64(E_im), 2, "e4m3")
    v_re = (er @ sr) - (ei @ si)
    v_im = (er @ si) + (ei @ sr)
    vr = mxq(v_re, 1, "e4m3")
    vi = mxq(v_im, 1, "e4m3")
    pr = mxq(f64(WPV_re), 1, "e4m3")
    pi = mxq(f64(WPV_im), 1, "e4m3")
    o_re = (pr @ vr) - (pi @ vi)
    o_im = (pr @ vi) + (pi @ vr)
    rho = np.maximum(np.arange(T, dtype=np.float64), 1.0)
    return o_re / rho[None, None, :], o_im / rho[None, None, :]

@@ -1,0 +1,275 @@
+from contextlib import ExitStack
+
+import concourse.mybir as mybir
+from concourse.masks import make_identity
+
+F32 = mybir.dt.float32
+BF16 = mybir.dt.bfloat16
+I32 = mybir.dt.int32
+U32 = mybir.dt.uint32
+U8 = mybir.dt.uint8
+FP8X4 = mybir.dt.float8_e4m3fn_x4
+ALU = mybir.AluOpType
+
+P = 128
+PACK = 4
+K_PASS = P * PACK
+T = 512
+D2 = 1024
+DIM = 512
+C_PASSES = D2 // K_PASS
+C_TILES = D2 // P
+O_TILES = DIM // P
+J_TILE = 128
+HALF = 256
+J_TILES_PER_HALF = HALF // J_TILE
+
+FLOPS = 2 * 4 * (D2 * T * T + DIM * D2 * T)
+
+PARTS = ("re", "im")
+V_TERMS = {"re": (("re", "re"), ("im", "neg_im")), "im": (("re", "im"), ("im", "re"))}
+OUT_TERMS = {"re": (("re", "re"), ("neg_im", "im")), "im": (("re", "im"), ("im", "re"))}
+
+
+def tile_autoregressivelsa_pb_kernel(
+    tc, E_re, E_im, S_re, S_im, WPV_re, WPV_im, out_0, out_1
+):
+    nc = tc.nc
+    ctx = ExitStack()
+    with ctx:
+        keep = ctx.enter_context(tc.tile_pool(name="keep", bufs=1))
+        stores = ctx.enter_context(tc.tile_pool(name="stores", bufs=4))
+        work = ctx.enter_context(tc.psum_pool(name="work", bufs=4))
+        sums = ctx.enter_context(tc.psum_pool(name="sums", bufs=4))
+
+        def mx_operand(name, words):
+            codes = keep.tile([P, words], U32, name=name + "_codes", align_bytes=64)
+            scales = keep.tile([P, words], U8, name=name + "_scales", align_bytes=64)
+            return codes, scales
+
+        def quantise(grouped, operand, first_word, words):
+            codes, scales = operand
+            nc.vector.quantize_mx(
+                out=codes[:, first_word : first_word + words].bitcast(FP8X4),
+                scales=scales[:, first_word : first_word + words],
+                in_=grouped[:, PACK * first_word : PACK * (first_word + words)],
+            )
+
+        def mx_pass(acc, stationary, m_word, moving, n_word, n_words, start, stop):
+            nc.tensor.matmul_mx(
+                out=acc,
+                lhsT=stationary[0][:, m_word : m_word + P].bitcast(FP8X4),
+                lhsT_scale=stationary[1][:, m_word : m_word + P],
+                rhs=moving[0][:, n_word : n_word + n_words].bitcast(FP8X4),
+                rhs_scale=moving[1][:, n_word : n_word + n_words],
+                start=start,
+                stop=stop,
+            )
+
+        e_raw = {}
+        s_raw = {}
+        w_raw = {}
+        e_grouped = {}
+        w_grouped = {}
+        s_grouped = {}
+        v_grouped = {}
+        e_mx = {}
+        w_mx = {}
+        s_mx = {}
+        v_mx = {}
+        for part in PARTS:
+            e_raw[part] = keep.tile([P, C_TILES, T], BF16, name="e_raw_" + part)
+            s_raw[part] = keep.tile([P, PACK, T], BF16, name="s_raw_" + part)
+            w_raw[part] = keep.tile([P, O_TILES, D2], BF16, name="w_raw_" + part)
+            e_grouped[part] = keep.tile(
+                [P, D2 * PACK], BF16, name="e_grouped_" + part, align_bytes=64
+            )
+            v_grouped[part] = keep.tile(
+                [P, C_PASSES * T * PACK], BF16, name="v_grouped_" + part, align_bytes=64
+            )
+            e_mx[part] = mx_operand("e_" + part, D2)
+            v_mx[part] = mx_operand("v_" + part, C_PASSES * T)
+        for part in PARTS + ("neg_im",):
+            s_grouped[part] = keep.tile(
+                [P, T * PACK], BF16, name="s_grouped_" + part, align_bytes=64
+            )
+            w_grouped[part] = keep.tile(
+                [P, C_PASSES * DIM * PACK], BF16, name="w_grouped_" + part, align_bytes=64
+            )
+            s_mx[part] = mx_operand("s_" + part, T)
+            w_mx[part] = mx_operand("w_" + part, C_PASSES * DIM)
+
+        e_dram = {"re": E_re, "im": E_im}
+        s_dram = {"re": S_re, "im": S_im}
+        w_dram = {"re": WPV_re, "im": WPV_im}
+
+        def load_scores(u):
+            first_j = u * HALF
+            for part in PARTS:
+                rows = s_dram[part].rearrange("b (u p e) j -> p (b u) e j", u=2, p=P, e=2)
+                nc.sync.dma_start(
+                    out=s_raw[part][:, 2 * u : 2 * u + 2, first_j:],
+                    in_=rows[:, u, :, first_j:],
+                )
+
+        def load_sequence(g):
+            for part in PARTS:
+                rows = e_dram[part].rearrange(
+                    "b (a p e) i -> p (b a) (e i)", a=2 * C_PASSES, p=P, e=2
+                )
+                tiles = e_raw[part][:].rearrange("p (a e) i -> p a (e i)", e=2)
+                nc.sync.dma_start(
+                    out=tiles[:, 2 * g : 2 * g + 2, :], in_=rows[:, 2 * g : 2 * g + 2, :]
+                )
+
+        for part in PARTS:
+            nc.vector.memset(s_raw[part][:, 2:4, 0:HALF], 0.0)
+        load_scores(0)
+        load_sequence(0)
+        load_sequence(1)
+        load_scores(1)
+        for part in PARTS:
+            nc.sync.dma_start(
+                out=w_raw[part][:], in_=w_dram[part].rearrange("(x p) c -> p x c", p=P)
+            )
+
+        distance = keep.tile([P, 2, HALF], I32, name="distance")
+        nc.gpsimd.iota(distance[:], pattern=[[-1, 2], [1, HALF]], base=0, channel_multiplier=-2)
+        keep_mask = keep.tile([P, 2, HALF], BF16, name="keep_mask")
+        nc.vector.tensor_scalar(
+            out=keep_mask[:], in0=distance[:], scalar1=0.0, scalar2=None, op0=ALU.is_ge
+        )
+        ident = keep.tile([P, P], F32, name="ident")
+        make_identity(nc, ident[:])
+        column = keep.tile([P, T], I32, name="column")
+        nc.gpsimd.iota(column[:], pattern=[[1, T]], base=0, channel_multiplier=0)
+        inv_rho = keep.tile([P, T], F32, name="inv_rho")
+
+        def prepare_scores(half):
+            cols = slice(half * HALF, (half + 1) * HALF)
+            for part in PARTS:
+                square = s_raw[part][:, 2 * half : 2 * half + 2, cols]
+                nc.vector.tensor_tensor(out=square, in0=square, in1=keep_mask[:], op=ALU.mult)
+            for part in PARTS:
+                nc.vector.tensor_copy(
+                    out=s_grouped[part][:].rearrange("p (j t) -> p j t", t=PACK)[:, cols, :],
+                    in_=s_raw[part][:, :, cols].rearrange("p t j -> p j t"),
+                )
+            quantise(s_grouped["re"], s_mx["re"], half * HALF, HALF)
+            values = slice(PACK * half * HALF, PACK * (half + 1) * HALF)
+            nc.vector.tensor_scalar_mul(
+                out=s_grouped["neg_im"][:, values], in0=s_grouped["im"][:, values], scalar1=-1.0
+            )
+            quantise(s_grouped["im"], s_mx["im"], half * HALF, HALF)
+            quantise(s_grouped["neg_im"], s_mx["neg_im"], half * HALF, HALF)
+
+        def transpose_words(two_blocks, grouped_words):
+            bank = work.tile([P, 2, 2, P], F32, tag="work")
+            for x in range(2):
+                for u in range(2):
+                    nc.tensor.transpose(
+                        bank[:, x, u, :], two_blocks[x][:, u * P : (u + 1) * P], ident[:]
+                    )
+            nc.scalar.copy(out=grouped_words, in_=bank[:].rearrange("p x u m -> p x m u"))
+
+        def transpose_sequence(g):
+            for part in PARTS:
+                words = e_grouped[part][:].bitcast(F32).rearrange(
+                    "p (c m u) -> p c m u", c=C_TILES, m=P, u=2
+                )
+                for c in range(PACK * g, PACK * (g + 1), 2):
+                    transpose_words(
+                        [e_raw[part][:, c + x, :].bitcast(F32) for x in range(2)],
+                        words[:, c : c + 2, :, :],
+                    )
+            for part in PARTS:
+                quantise(e_grouped[part], e_mx[part], g * K_PASS, K_PASS)
+
+        def transpose_weights(g):
+            for part in PARTS:
+                words = w_grouped[part][:].bitcast(F32).rearrange(
+                    "p (g x m u) -> p g x m u", g=C_PASSES, x=O_TILES, m=P, u=2
+                )
+                pass_words = slice(g * K_PASS // 2, (g + 1) * K_PASS // 2)
+                for o in range(0, O_TILES, 2):
+                    transpose_words(
+                        [w_raw[part][:, o + x, :].bitcast(F32)[:, pass_words] for x in range(2)],
+                        words[:, g, o : o + 2, :, :],
+                    )
+            values = slice(PACK * g * DIM, PACK * (g + 1) * DIM)
+            quantise(w_grouped["re"], w_mx["re"], g * DIM, DIM)
+            nc.vector.tensor_scalar_mul(
+                out=w_grouped["neg_im"][:, values], in0=w_grouped["im"][:, values], scalar1=-1.0
+            )
+            quantise(w_grouped["im"], w_mx["im"], g * DIM, DIM)
+            quantise(w_grouped["neg_im"], w_mx["neg_im"], g * DIM, DIM)
+
+        def first_stage(half):
+            for g in range(C_PASSES):
+                for part in PARTS:
+                    grouped = v_grouped[part][:].rearrange(
+                        "p (g j t) -> p g j t", g=C_PASSES, j=T, t=PACK
+                    )
+                    for jt in range(half * J_TILES_PER_HALF, (half + 1) * J_TILES_PER_HALF):
+                        bank = work.tile([P, PACK, J_TILE], F32, tag="work")
+                        for t in range(PACK):
+                            for n, (e_part, s_part) in enumerate(V_TERMS[part]):
+                                mx_pass(
+                                    bank[:, t, :],
+                                    e_mx[e_part],
+                                    (PACK * g + t) * P,
+                                    s_mx[s_part],
+                                    jt * J_TILE,
+                                    J_TILE,
+                                    start=(n == 0),
+                                    stop=(n == 1),
+                                )
+                        nc.scalar.copy(
+                            out=grouped[:, g, jt * J_TILE : (jt + 1) * J_TILE, :],
+                            in_=bank[:].rearrange("p t j -> p j t"),
+                        )
+                    quantise(v_grouped[part], v_mx[part], g * T + half * HALF, HALF)
+
+        def second_stage(half):
+            cols = slice(half * HALF, (half + 1) * HALF)
+            out_dram = {"re": out_0, "im": out_1}
+            for o in range(O_TILES):
+                bank = sums.tile([P, 2, HALF], F32, tag="sums")
+                for y, part in enumerate(PARTS):
+                    terms = [(g, w, v) for g in range(C_PASSES) for (w, v) in OUT_TERMS[part]]
+                    for n, (g, w_part, v_part) in enumerate(terms):
+                        mx_pass(
+                            bank[:, y, :],
+                            w_mx[w_part],
+                            g * DIM + o * P,
+                            v_mx[v_part],
+                            g * T + half * HALF,
+                            HALF,
+                            start=(n == 0),
+                            stop=(n == len(terms) - 1),
+                        )
+                scaled = stores.tile([P, 2, HALF], F32, tag="scaled")
+                nc.vector.tensor_tensor(
+                    out=scaled[:],
+                    in0=bank[:],
+                    in1=inv_rho[:, cols].unsqueeze(1).to_broadcast([P, 2, HALF]),
+                    op=ALU.mult,
+                )
+                for y, part in enumerate(PARTS):
+                    rows = out_dram[part].rearrange("b (x p) j -> p (b x) j", p=P)
+                    nc.sync.dma_start(out=rows[:, o, cols], in_=scaled[:, y, :])
+
+        prepare_scores(0)
+        transpose_sequence(0)
+        transpose_sequence(1)
+        prepare_scores(1)
+        nc.vector.tensor_scalar(
+            out=inv_rho[:], in0=column[:], scalar1=1.0, scalar2=None, op0=ALU.max
+        )
+        nc.vector.reciprocal(out=inv_rho[:], in_=inv_rho[:])
+        first_stage(0)
+        transpose_weights(0)
+        transpose_weights(1)
+        first_stage(1)
+        second_stage(0)
+        second_stage(1)

@@ -20,6 +20,7 @@ DIM = 512
 C_PASSES = D2 // K_PASS
 C_TILES = D2 // P
 O_TILES = DIM // P
+O_PAIRS = O_TILES // 2
 J_TILE = 128
 HALF = 256
 J_TILES_PER_HALF = HALF // J_TILE
@@ -41,6 +42,7 @@ def tile_autoregressivelsa_pb_kernel(
         stores = ctx.enter_context(tc.tile_pool(name="stores", bufs=4))
         work = ctx.enter_context(tc.psum_pool(name="work", bufs=4))
         sums = ctx.enter_context(tc.psum_pool(name="sums", bufs=4))
+        ctx.enter_context(tc.manual_schedule())
 
         def mx_operand(name, words):
             codes = keep.tile([P, words], U32, name=name + "_codes", align_bytes=64)
@@ -103,13 +105,12 @@ def tile_autoregressivelsa_pb_kernel(
         s_dram = {"re": S_re, "im": S_im}
         w_dram = {"re": WPV_re, "im": WPV_im}
 
-        def load_scores(u):
-            first_j = u * HALF
+        def load_scores(u, half):
+            cols = slice(half * HALF, (half + 1) * HALF)
             for part in PARTS:
                 rows = s_dram[part].rearrange("b (u p e) j -> p (b u) e j", u=2, p=P, e=2)
                 nc.sync.dma_start(
-                    out=s_raw[part][:, 2 * u : 2 * u + 2, first_j:],
-                    in_=rows[:, u, :, first_j:],
+                    out=s_raw[part][:, 2 * u : 2 * u + 2, cols], in_=rows[:, u, :, cols]
                 )
 
         def load_sequence(g):
@@ -124,13 +125,15 @@ def tile_autoregressivelsa_pb_kernel(
 
         for part in PARTS:
             nc.vector.memset(s_raw[part][:, 2:4, 0:HALF], 0.0)
-        load_scores(0)
+        load_scores(0, 0)
         load_sequence(0)
         load_sequence(1)
-        load_scores(1)
+        load_scores(0, 1)
+        load_scores(1, 1)
         for part in PARTS:
             nc.sync.dma_start(
-                out=w_raw[part][:], in_=w_dram[part].rearrange("(x p) c -> p x c", p=P)
+                out=w_raw[part][:].rearrange("m x c -> m (x c)"),
+                in_=w_dram[part].rearrange("(m x) c -> m (x c)", x=O_TILES),
             )
 
         distance = keep.tile([P, 2, HALF], I32, name="distance")
@@ -139,11 +142,26 @@ def tile_autoregressivelsa_pb_kernel(
         nc.vector.tensor_scalar(
             out=keep_mask[:], in0=distance[:], scalar1=0.0, scalar2=None, op0=ALU.is_ge
         )
+        column = keep.tile([P, T // P], I32, name="column")
+        nc.gpsimd.iota(column[:], pattern=[[P, T // P]], base=0, channel_multiplier=1)
+        inv_rho_column = keep.tile([P, T // P], F32, name="inv_rho_column")
+        nc.vector.tensor_scalar(
+            out=inv_rho_column[:], in0=column[:], scalar1=1.0, scalar2=None, op0=ALU.max
+        )
+        nc.vector.reciprocal(out=inv_rho_column[:], in_=inv_rho_column[:])
         ident = keep.tile([P, P], F32, name="ident")
         make_identity(nc, ident[:])
-        column = keep.tile([P, T], I32, name="column")
-        nc.gpsimd.iota(column[:], pattern=[[1, T]], base=0, channel_multiplier=0)
+        spread = work.tile([P, T // P, P], F32, tag="work")
+        for n in range(T // P):
+            nc.tensor.matmul(
+                out=spread[:, n, :],
+                lhsT=inv_rho_column[:, n : n + 1].to_broadcast([P, P]),
+                rhs=ident[:],
+                start=True,
+                stop=True,
+            )
         inv_rho = keep.tile([P, T], F32, name="inv_rho")
+        nc.scalar.copy(out=inv_rho[:], in_=spread[:].rearrange("m n p -> m (n p)"))
 
         def prepare_scores(half):
             cols = slice(half * HALF, (half + 1) * HALF)
@@ -152,8 +170,10 @@ def tile_autoregressivelsa_pb_kernel(
                 nc.vector.tensor_tensor(out=square, in0=square, in1=keep_mask[:], op=ALU.mult)
             for part in PARTS:
                 nc.vector.tensor_copy(
-                    out=s_grouped[part][:].rearrange("p (j t) -> p j t", t=PACK)[:, cols, :],
-                    in_=s_raw[part][:, :, cols].rearrange("p t j -> p j t"),
+                    out=s_grouped[part][:]
+                    .rearrange("p (j t) -> p j t", t=PACK)[:, cols, :]
+                    .rearrange("p (c r) t -> p c t r", r=4),
+                    in_=s_raw[part][:, :, cols].rearrange("p t (c r) -> p c t r", r=4),
                 )
             quantise(s_grouped["re"], s_mx["re"], half * HALF, HALF)
             values = slice(PACK * half * HALF, PACK * (half + 1) * HALF)
@@ -163,14 +183,18 @@ def tile_autoregressivelsa_pb_kernel(
             quantise(s_grouped["im"], s_mx["im"], half * HALF, HALF)
             quantise(s_grouped["neg_im"], s_mx["neg_im"], half * HALF, HALF)
 
-        def transpose_words(two_blocks, grouped_words):
-            bank = work.tile([P, 2, 2, P], F32, tag="work")
+        def transpose_words(bank, two_blocks, grouped_words, on_vector):
             for x in range(2):
                 for u in range(2):
                     nc.tensor.transpose(
                         bank[:, x, u, :], two_blocks[x][:, u * P : (u + 1) * P], ident[:]
                     )
-            nc.scalar.copy(out=grouped_words, in_=bank[:].rearrange("p x u m -> p x m u"))
+            if on_vector:
+                nc.vector.tensor_copy(
+                    out=grouped_words, in_=bank[:].rearrange("p x u m -> p x m u")
+                )
+            else:
+                nc.scalar.copy(out=grouped_words, in_=bank[:].rearrange("p x u m -> p x m u"))
 
         def transpose_sequence(g):
             for part in PARTS:
@@ -178,98 +202,116 @@ def tile_autoregressivelsa_pb_kernel(
                     "p (c m u) -> p c m u", c=C_TILES, m=P, u=2
                 )
                 for c in range(PACK * g, PACK * (g + 1), 2):
+                    bank = work.tile([P, 2, 2, P], F32, tag="work")
                     transpose_words(
+                        bank,
                         [e_raw[part][:, c + x, :].bitcast(F32) for x in range(2)],
                         words[:, c : c + 2, :, :],
+                        on_vector=False,
                     )
             for part in PARTS:
                 quantise(e_grouped[part], e_mx[part], g * K_PASS, K_PASS)
 
-        def transpose_weights(g):
-            for part in PARTS:
-                words = w_grouped[part][:].bitcast(F32).rearrange(
-                    "p (g x m u) -> p g x m u", g=C_PASSES, x=O_TILES, m=P, u=2
-                )
-                pass_words = slice(g * K_PASS // 2, (g + 1) * K_PASS // 2)
-                for o in range(0, O_TILES, 2):
-                    transpose_words(
-                        [w_raw[part][:, o + x, :].bitcast(F32)[:, pass_words] for x in range(2)],
-                        words[:, g, o : o + 2, :, :],
-                    )
-            values = slice(PACK * g * DIM, PACK * (g + 1) * DIM)
-            quantise(w_grouped["re"], w_mx["re"], g * DIM, DIM)
-            nc.vector.tensor_scalar_mul(
-                out=w_grouped["neg_im"][:, values], in0=w_grouped["im"][:, values], scalar1=-1.0
-            )
-            quantise(w_grouped["im"], w_mx["im"], g * DIM, DIM)
-            quantise(w_grouped["neg_im"], w_mx["neg_im"], g * DIM, DIM)
+        def weight_word(pair, g, x):
+            return ((pair * C_PASSES + g) * 2 + x) * P
 
-        def first_stage(half):
-            for g in range(C_PASSES):
-                for part in PARTS:
-                    grouped = v_grouped[part][:].rearrange(
-                        "p (g j t) -> p g j t", g=C_PASSES, j=T, t=PACK
+        def transpose_weights(part):
+            words = w_grouped[part][:].bitcast(F32).rearrange(
+                "p (b x m u) -> p b x m u", b=O_PAIRS * C_PASSES, x=2, m=P, u=2
+            )
+            for pair in range(O_PAIRS):
+                for g in range(C_PASSES):
+                    pass_words = slice(g * K_PASS // 2, (g + 1) * K_PASS // 2)
+                    bank = sums.tile([P, 2, 2, P], F32, tag="sums")
+                    transpose_words(
+                        bank,
+                        [
+                            w_raw[part][:, 2 * pair + x, :].bitcast(F32)[:, pass_words]
+                            for x in range(2)
+                        ],
+                        words[:, pair * C_PASSES + g, :, :, :],
+                        on_vector=(g == 1),
                     )
-                    for jt in range(half * J_TILES_PER_HALF, (half + 1) * J_TILES_PER_HALF):
-                        bank = work.tile([P, PACK, J_TILE], F32, tag="work")
-                        for t in range(PACK):
-                            for n, (e_part, s_part) in enumerate(V_TERMS[part]):
-                                mx_pass(
-                                    bank[:, t, :],
-                                    e_mx[e_part],
-                                    (PACK * g + t) * P,
-                                    s_mx[s_part],
-                                    jt * J_TILE,
-                                    J_TILE,
-                                    start=(n == 0),
-                                    stop=(n == 1),
-                                )
-                        nc.scalar.copy(
-                            out=grouped[:, g, jt * J_TILE : (jt + 1) * J_TILE, :],
-                            in_=bank[:].rearrange("p t j -> p j t"),
-                        )
-                    quantise(v_grouped[part], v_mx[part], g * T + half * HALF, HALF)
+                first = weight_word(pair, 0, 0)
+                count = C_PASSES * 2 * P
+                if part == "im":
+                    values = slice(PACK * first, PACK * (first + count))
+                    nc.vector.tensor_scalar_mul(
+                        out=w_grouped["neg_im"][:, values],
+                        in0=w_grouped["im"][:, values],
+                        scalar1=-1.0,
+                    )
+                    quantise(w_grouped["im"], w_mx["im"], first, count)
+                    quantise(w_grouped["neg_im"], w_mx["neg_im"], first, count)
+                else:
+                    quantise(w_grouped["re"], w_mx["re"], first, count)
+
+        def first_stage(half, g):
+            for part in PARTS:
+                grouped = v_grouped[part][:].rearrange(
+                    "p (g j t) -> p g j t", g=C_PASSES, j=T, t=PACK
+                )
+                for jt in range(half * J_TILES_PER_HALF, (half + 1) * J_TILES_PER_HALF):
+                    bank = work.tile([P, PACK, J_TILE], F32, tag="work")
+                    for t in range(PACK):
+                        for n, (e_part, s_part) in enumerate(V_TERMS[part]):
+                            mx_pass(
+                                bank[:, t, :],
+                                e_mx[e_part],
+                                (PACK * g + t) * P,
+                                s_mx[s_part],
+                                jt * J_TILE,
+                                J_TILE,
+                                start=(n == 0),
+                                stop=(n == 1),
+                            )
+                    nc.scalar.copy(
+                        out=grouped[:, g, jt * J_TILE : (jt + 1) * J_TILE, :],
+                        in_=bank[:].rearrange("p t j -> p j t"),
+                    )
+                quantise(v_grouped[part], v_mx[part], g * T + half * HALF, HALF)
 
         def second_stage(half):
             cols = slice(half * HALF, (half + 1) * HALF)
             out_dram = {"re": out_0, "im": out_1}
-            for o in range(O_TILES):
-                bank = sums.tile([P, 2, HALF], F32, tag="sums")
-                for y, part in enumerate(PARTS):
-                    terms = [(g, w, v) for g in range(C_PASSES) for (w, v) in OUT_TERMS[part]]
-                    for n, (g, w_part, v_part) in enumerate(terms):
-                        mx_pass(
-                            bank[:, y, :],
-                            w_mx[w_part],
-                            g * DIM + o * P,
-                            v_mx[v_part],
-                            g * T + half * HALF,
-                            HALF,
-                            start=(n == 0),
-                            stop=(n == len(terms) - 1),
-                        )
-                scaled = stores.tile([P, 2, HALF], F32, tag="scaled")
-                nc.vector.tensor_tensor(
-                    out=scaled[:],
-                    in0=bank[:],
-                    in1=inv_rho[:, cols].unsqueeze(1).to_broadcast([P, 2, HALF]),
-                    op=ALU.mult,
-                )
-                for y, part in enumerate(PARTS):
-                    rows = out_dram[part].rearrange("b (x p) j -> p (b x) j", p=P)
-                    nc.sync.dma_start(out=rows[:, o, cols], in_=scaled[:, y, :])
+            for pair in range(O_PAIRS):
+                for x in range(2):
+                    bank = sums.tile([P, 2, HALF], F32, tag="sums")
+                    for y, part in enumerate(PARTS):
+                        terms = [
+                            (g, w, v) for g in range(C_PASSES) for (w, v) in OUT_TERMS[part]
+                        ]
+                        for n, (g, w_part, v_part) in enumerate(terms):
+                            mx_pass(
+                                bank[:, y, :],
+                                w_mx[w_part],
+                                weight_word(pair, g, x),
+                                v_mx[v_part],
+                                g * T + half * HALF,
+                                HALF,
+                                start=(n == 0),
+                                stop=(n == len(terms) - 1),
+                            )
+                    scaled = stores.tile([P, 2, HALF], F32, tag="scaled")
+                    nc.vector.tensor_tensor(
+                        out=scaled[:],
+                        in0=bank[:],
+                        in1=inv_rho[:, cols].unsqueeze(1).to_broadcast([P, 2, HALF]),
+                        op=ALU.mult,
+                    )
+                    for y, part in enumerate(PARTS):
+                        rows = out_dram[part].rearrange("b (m x) j -> m (b x) j", x=O_TILES)
+                        nc.sync.dma_start(out=rows[:, 2 * pair + x, cols], in_=scaled[:, y, :])
 
         prepare_scores(0)
         transpose_sequence(0)
         transpose_sequence(1)
         prepare_scores(1)
-        nc.vector.tensor_scalar(
-            out=inv_rho[:], in0=column[:], scalar1=1.0, scalar2=None, op0=ALU.max
-        )
-        nc.vector.reciprocal(out=inv_rho[:], in_=inv_rho[:])
-        first_stage(0)
-        transpose_weights(0)
-        transpose_weights(1)
-        first_stage(1)
+        first_stage(0, 0)
+        first_stage(0, 1)
+        transpose_weights("re")
+        first_stage(1, 0)
+        transpose_weights("im")
+        first_stage(1, 1)
         second_stage(0)
         second_stage(1)

@@ -39,9 +39,8 @@ def tile_autoregressivelsa_pb_kernel(
     ctx = ExitStack()
     with ctx:
         keep = ctx.enter_context(tc.tile_pool(name="keep", bufs=1))
-        stores = ctx.enter_context(tc.tile_pool(name="stores", bufs=4))
-        work = ctx.enter_context(tc.psum_pool(name="work", bufs=4))
-        sums = ctx.enter_context(tc.psum_pool(name="sums", bufs=4))
+        stores = ctx.enter_context(tc.tile_pool(name="stores", bufs=8))
+        banks = ctx.enter_context(tc.psum_pool(name="banks", bufs=8))
         ctx.enter_context(tc.manual_schedule())
 
         def mx_operand(name, words):
@@ -136,12 +135,6 @@ def tile_autoregressivelsa_pb_kernel(
                 in_=w_dram[part].rearrange("(m x) c -> m (x c)", x=O_TILES),
             )
 
-        distance = keep.tile([P, 2, HALF], I32, name="distance")
-        nc.gpsimd.iota(distance[:], pattern=[[-1, 2], [1, HALF]], base=0, channel_multiplier=-2)
-        keep_mask = keep.tile([P, 2, HALF], BF16, name="keep_mask")
-        nc.vector.tensor_scalar(
-            out=keep_mask[:], in0=distance[:], scalar1=0.0, scalar2=None, op0=ALU.is_ge
-        )
         column = keep.tile([P, T // P], I32, name="column")
         nc.gpsimd.iota(column[:], pattern=[[P, T // P]], base=0, channel_multiplier=1)
         inv_rho_column = keep.tile([P, T // P], F32, name="inv_rho_column")
@@ -151,7 +144,7 @@ def tile_autoregressivelsa_pb_kernel(
         nc.vector.reciprocal(out=inv_rho_column[:], in_=inv_rho_column[:])
         ident = keep.tile([P, P], F32, name="ident")
         make_identity(nc, ident[:])
-        spread = work.tile([P, T // P, P], F32, tag="work")
+        spread = banks.tile([P, T // P, P], F32, tag="bank")
         for n in range(T // P):
             nc.tensor.matmul(
                 out=spread[:, n, :],
@@ -162,6 +155,12 @@ def tile_autoregressivelsa_pb_kernel(
             )
         inv_rho = keep.tile([P, T], F32, name="inv_rho")
         nc.scalar.copy(out=inv_rho[:], in_=spread[:].rearrange("m n p -> m (n p)"))
+        distance = keep.tile([P, 2, HALF], I32, name="distance")
+        nc.gpsimd.iota(distance[:], pattern=[[-1, 2], [1, HALF]], base=0, channel_multiplier=-2)
+        keep_mask = keep.tile([P, 2, HALF], BF16, name="keep_mask")
+        nc.vector.tensor_scalar(
+            out=keep_mask[:], in0=distance[:], scalar1=0.0, scalar2=None, op0=ALU.is_ge
+        )
 
         def prepare_scores(half):
             cols = slice(half * HALF, (half + 1) * HALF)
@@ -202,7 +201,7 @@ def tile_autoregressivelsa_pb_kernel(
                     "p (c m u) -> p c m u", c=C_TILES, m=P, u=2
                 )
                 for c in range(PACK * g, PACK * (g + 1), 2):
-                    bank = work.tile([P, 2, 2, P], F32, tag="work")
+                    bank = banks.tile([P, 2, 2, P], F32, tag="bank")
                     transpose_words(
                         bank,
                         [e_raw[part][:, c + x, :].bitcast(F32) for x in range(2)],
@@ -222,7 +221,7 @@ def tile_autoregressivelsa_pb_kernel(
             for pair in range(O_PAIRS):
                 for g in range(C_PASSES):
                     pass_words = slice(g * K_PASS // 2, (g + 1) * K_PASS // 2)
-                    bank = sums.tile([P, 2, 2, P], F32, tag="sums")
+                    bank = banks.tile([P, 2, 2, P], F32, tag="bank")
                     transpose_words(
                         bank,
                         [
@@ -252,7 +251,7 @@ def tile_autoregressivelsa_pb_kernel(
                     "p (g j t) -> p g j t", g=C_PASSES, j=T, t=PACK
                 )
                 for jt in range(half * J_TILES_PER_HALF, (half + 1) * J_TILES_PER_HALF):
-                    bank = work.tile([P, PACK, J_TILE], F32, tag="work")
+                    bank = banks.tile([P, PACK, J_TILE], F32, tag="bank")
                     for t in range(PACK):
                         for n, (e_part, s_part) in enumerate(V_TERMS[part]):
                             mx_pass(
@@ -276,14 +275,14 @@ def tile_autoregressivelsa_pb_kernel(
             out_dram = {"re": out_0, "im": out_1}
             for pair in range(O_PAIRS):
                 for x in range(2):
-                    bank = sums.tile([P, 2, HALF], F32, tag="sums")
-                    for y, part in enumerate(PARTS):
+                    for part in PARTS:
+                        acc = banks.tile([P, HALF], F32, tag="bank")
                         terms = [
                             (g, w, v) for g in range(C_PASSES) for (w, v) in OUT_TERMS[part]
                         ]
                         for n, (g, w_part, v_part) in enumerate(terms):
                             mx_pass(
-                                bank[:, y, :],
+                                acc[:],
                                 w_mx[w_part],
                                 weight_word(pair, g, x),
                                 v_mx[v_part],
@@ -292,16 +291,12 @@ def tile_autoregressivelsa_pb_kernel(
                                 start=(n == 0),
                                 stop=(n == len(terms) - 1),
                             )
-                    scaled = stores.tile([P, 2, HALF], F32, tag="scaled")
-                    nc.vector.tensor_tensor(
-                        out=scaled[:],
-                        in0=bank[:],
-                        in1=inv_rho[:, cols].unsqueeze(1).to_broadcast([P, 2, HALF]),
-                        op=ALU.mult,
-                    )
-                    for y, part in enumerate(PARTS):
+                        scaled = stores.tile([P, HALF], F32, tag="scaled")
+                        nc.vector.tensor_tensor(
+                            out=scaled[:], in0=acc[:], in1=inv_rho[:, cols], op=ALU.mult
+                        )
                         rows = out_dram[part].rearrange("b (m x) j -> m (b x) j", x=O_TILES)
-                        nc.sync.dma_start(out=rows[:, 2 * pair + x, cols], in_=scaled[:, y, :])
+                        nc.sync.dma_start(out=rows[:, 2 * pair + x, cols], in_=scaled[:])
 
         prepare_scores(0)
         transpose_sequence(0)

@@ -29,7 +29,7 @@ FLOPS = 2 * 4 * (D2 * T * T + DIM * D2 * T)
 
 PARTS = ("re", "im")
 V_TERMS = {"re": (("re", "re"), ("im", "neg_im")), "im": (("re", "im"), ("im", "re"))}
-OUT_TERMS = {"re": (("re", "re"), ("neg_im", "im")), "im": (("re", "im"), ("im", "re"))}
+OUT_TERMS = {"re": (("re", "re"), ("im", "im")), "im": (("re", "im"), ("im", "re"))}
 
 
 def tile_autoregressivelsa_pb_kernel(
@@ -94,10 +94,11 @@ def tile_autoregressivelsa_pb_kernel(
             s_grouped[part] = keep.tile(
                 [P, T * PACK], BF16, name="s_grouped_" + part, align_bytes=64
             )
+            s_mx[part] = mx_operand("s_" + part, T)
+        for part in PARTS:
             w_grouped[part] = keep.tile(
                 [P, C_PASSES * DIM * PACK], BF16, name="w_grouped_" + part, align_bytes=64
             )
-            s_mx[part] = mx_operand("s_" + part, T)
             w_mx[part] = mx_operand("w_" + part, C_PASSES * DIM)
 
         e_dram = {"re": E_re, "im": E_im}
@@ -233,17 +234,7 @@ def tile_autoregressivelsa_pb_kernel(
                     )
                 first = weight_word(pair, 0, 0)
                 count = C_PASSES * 2 * P
-                if part == "im":
-                    values = slice(PACK * first, PACK * (first + count))
-                    nc.vector.tensor_scalar_mul(
-                        out=w_grouped["neg_im"][:, values],
-                        in0=w_grouped["im"][:, values],
-                        scalar1=-1.0,
-                    )
-                    quantise(w_grouped["im"], w_mx["im"], first, count)
-                    quantise(w_grouped["neg_im"], w_mx["neg_im"], first, count)
-                else:
-                    quantise(w_grouped["re"], w_mx["re"], first, count)
+                quantise(w_grouped[part], w_mx[part], first, count)
 
         def first_stage(half, g):
             for part in PARTS:
@@ -273,30 +264,47 @@ def tile_autoregressivelsa_pb_kernel(
         def second_stage(half):
             cols = slice(half * HALF, (half + 1) * HALF)
             out_dram = {"re": out_0, "im": out_1}
+            def add_up(acc, pair, x, terms):
+                passes = [(g, w, v) for g in range(C_PASSES) for (w, v) in terms]
+                for n, (g, w_part, v_part) in enumerate(passes):
+                    mx_pass(
+                        acc,
+                        w_mx[w_part],
+                        weight_word(pair, g, x),
+                        v_mx[v_part],
+                        g * T + half * HALF,
+                        HALF,
+                        start=(n == 0),
+                        stop=(n == len(passes) - 1),
+                    )
+
+            def store(part, pair, x, scaled):
+                rows = out_dram[part].rearrange("b (m x) j -> m (b x) j", x=O_TILES)
+                nc.sync.dma_start(out=rows[:, 2 * pair + x, cols], in_=scaled[:])
+
             for pair in range(O_PAIRS):
                 for x in range(2):
-                    for part in PARTS:
-                        acc = banks.tile([P, HALF], F32, tag="bank")
-                        terms = [
-                            (g, w, v) for g in range(C_PASSES) for (w, v) in OUT_TERMS[part]
-                        ]
-                        for n, (g, w_part, v_part) in enumerate(terms):
-                            mx_pass(
-                                acc[:],
-                                w_mx[w_part],
-                                weight_word(pair, g, x),
-                                v_mx[v_part],
-                                g * T + half * HALF,
-                                HALF,
-                                start=(n == 0),
-                                stop=(n == len(terms) - 1),
-                            )
-                        scaled = stores.tile([P, HALF], F32, tag="scaled")
-                        nc.vector.tensor_tensor(
-                            out=scaled[:], in0=acc[:], in1=inv_rho[:, cols], op=ALU.mult
-                        )
-                        rows = out_dram[part].rearrange("b (m x) j -> m (b x) j", x=O_TILES)
-                        nc.sync.dma_start(out=rows[:, 2 * pair + x, cols], in_=scaled[:])
+                    bank = banks.tile([P, 2, HALF], F32, tag="bank")
+                    for n, term in enumerate(OUT_TERMS["re"]):
+                        add_up(bank[:, n, :], pair, x, [term])
+                    acc = banks.tile([P, HALF], F32, tag="bank")
+                    add_up(acc[:], pair, x, OUT_TERMS["im"])
+                    subtrahend = stores.tile([P, HALF], F32, tag="subtrahend")
+                    nc.scalar.copy(out=subtrahend[:], in_=bank[:, 1, :])
+                    difference = stores.tile([P, HALF], F32, tag="difference")
+                    nc.vector.tensor_tensor(
+                        out=difference[:], in0=bank[:, 0, :], in1=subtrahend[:], op=ALU.subtract
+                    )
+                    scaled_im = stores.tile([P, HALF], F32, tag="scaled")
+                    nc.vector.tensor_tensor(
+                        out=scaled_im[:], in0=acc[:], in1=inv_rho[:, cols], op=ALU.mult
+                    )
+                    scaled_re = stores.tile([P, HALF], F32, tag="scaled")
+                    nc.vector.tensor_tensor(
+                        out=scaled_re[:], in0=difference[:], in1=inv_rho[:, cols], op=ALU.mult
+                    )
+                    store("im", pair, x, scaled_im)
+                    store("re", pair, x, scaled_re)
 
         prepare_scores(0)
         transpose_sequence(0)

@@ -123,6 +123,9 @@ def tile_autoregressivelsa_pb_kernel(
                     out=tiles[:, 2 * g : 2 * g + 2, :], in_=rows[:, 2 * g : 2 * g + 2, :]
                 )
 
+        zeros = keep.tile([P, T], BF16, name="zeros")
+        nc.vector.memset(zeros[:].bitcast(I32), 0)
+
         for part in PARTS:
             nc.vector.memset(s_raw[part][:, 2:4, 0:HALF], 0.0)
         load_scores(0, 0)
@@ -136,6 +139,13 @@ def tile_autoregressivelsa_pb_kernel(
                 in_=w_dram[part].rearrange("(m x) c -> m (x c)", x=O_TILES),
             )
 
+        def keep_warm(count):
+            bank = banks.tile([P, T], F32, tag="bank")
+            for n in range(count):
+                nc.tensor.matmul(
+                    out=bank[:], lhsT=zeros[:, 0:P], rhs=zeros[:], start=True, stop=True
+                )
+
         column = keep.tile([P, T // P], I32, name="column")
         nc.gpsimd.iota(column[:], pattern=[[P, T // P]], base=0, channel_multiplier=1)
         inv_rho_column = keep.tile([P, T // P], F32, name="inv_rho_column")
@@ -145,6 +155,7 @@ def tile_autoregressivelsa_pb_kernel(
         nc.vector.reciprocal(out=inv_rho_column[:], in_=inv_rho_column[:])
         ident = keep.tile([P, P], F32, name="ident")
         make_identity(nc, ident[:])
+        keep_warm(2)
         spread = banks.tile([P, T // P, P], F32, tag="bank")
         for n in range(T // P):
             nc.tensor.matmul(
@@ -154,6 +165,7 @@ def tile_autoregressivelsa_pb_kernel(
                 start=True,
                 stop=True,
             )
+        keep_warm(2)
         inv_rho = keep.tile([P, T], F32, name="inv_rho")
         nc.scalar.copy(out=inv_rho[:], in_=spread[:].rearrange("m n p -> m (n p)"))
         distance = keep.tile([P, 2, HALF], I32, name="distance")
@@ -198,6 +210,8 @@ def tile_autoregressivelsa_pb_kernel(
 
         def transpose_sequence(g):
             for part in PARTS:
+                if (g, part) != (0, "re"):
+                    keep_warm(1)
                 words = e_grouped[part][:].bitcast(F32).rearrange(
                     "p (c m u) -> p c m u", c=C_TILES, m=P, u=2
                 )

@@ -298,16 +298,18 @@ def tile_autoregressivelsa_pb_kernel(
 
             for pair in range(O_PAIRS):
                 for x in range(2):
-                    bank = banks.tile([P, 2, HALF], F32, tag="bank")
-                    for n, term in enumerate(OUT_TERMS["re"]):
-                        add_up(bank[:, n, :], pair, x, [term])
+                    minuend_term, subtrahend_term = OUT_TERMS["re"]
+                    bank = banks.tile([P, HALF], F32, tag="bank")
+                    add_up(bank[:], pair, x, [subtrahend_term])
+                    minuend = banks.tile([P, HALF], F32, tag="bank")
+                    add_up(minuend[:], pair, x, [minuend_term])
                     acc = banks.tile([P, HALF], F32, tag="bank")
                     add_up(acc[:], pair, x, OUT_TERMS["im"])
                     subtrahend = stores.tile([P, HALF], F32, tag="subtrahend")
-                    nc.scalar.copy(out=subtrahend[:], in_=bank[:, 1, :])
+                    nc.scalar.copy(out=subtrahend[:], in_=bank[:])
                     difference = stores.tile([P, HALF], F32, tag="difference")
                     nc.vector.tensor_tensor(
-                        out=difference[:], in0=bank[:, 0, :], in1=subtrahend[:], op=ALU.subtract
+                        out=difference[:], in0=minuend[:], in1=subtrahend[:], op=ALU.subtract
                     )
                     scaled_im = stores.tile([P, HALF], F32, tag="scaled")
                     nc.vector.tensor_tensor(

from contextlib import ExitStack

import concourse.mybir as mybir
from concourse.masks import make_identity

F32 = mybir.dt.float32
BF16 = mybir.dt.bfloat16
I32 = mybir.dt.int32
U32 = mybir.dt.uint32
U8 = mybir.dt.uint8
FP8X4 = mybir.dt.float8_e4m3fn_x4
ALU = mybir.AluOpType

P = 128
PACK = 4
K_PASS = P * PACK
T = 512
D2 = 1024
DIM = 512
C_PASSES = D2 // K_PASS
C_TILES = D2 // P
O_TILES = DIM // P
O_PAIRS = O_TILES // 2
J_TILE = 128
HALF = 256
J_TILES_PER_HALF = HALF // J_TILE

FLOPS = 2 * 4 * (D2 * T * T + DIM * D2 * T)

PARTS = ("re", "im")
V_TERMS = {"re": (("re", "re"), ("im", "neg_im")), "im": (("re", "im"), ("im", "re"))}
OUT_TERMS = {"re": (("re", "re"), ("im", "im")), "im": (("re", "im"), ("im", "re"))}


def tile_autoregressivelsa_pb_kernel(
    tc, E_re, E_im, S_re, S_im, WPV_re, WPV_im, out_0, out_1
):
    nc = tc.nc
    ctx = ExitStack()
    with ctx:
        keep = ctx.enter_context(tc.tile_pool(name="keep", bufs=1))
        stores = ctx.enter_context(tc.tile_pool(name="stores", bufs=8))
        banks = ctx.enter_context(tc.psum_pool(name="banks", bufs=8))
        ctx.enter_context(tc.manual_schedule())

        def mx_operand(name, words):
            codes = keep.tile([P, words], U32, name=name + "_codes", align_bytes=64)
            scales = keep.tile([P, words], U8, name=name + "_scales", align_bytes=64)
            return codes, scales

        def quantise(grouped, operand, first_word, words):
            codes, scales = operand
            nc.vector.quantize_mx(
                out=codes[:, first_word : first_word + words].bitcast(FP8X4),
                scales=scales[:, first_word : first_word + words],
                in_=grouped[:, PACK * first_word : PACK * (first_word + words)],
            )

        def mx_pass(acc, stationary, m_word, moving, n_word, n_words, start, stop):
            nc.tensor.matmul_mx(
                out=acc,
                lhsT=stationary[0][:, m_word : m_word + P].bitcast(FP8X4),
                lhsT_scale=stationary[1][:, m_word : m_word + P],
                rhs=moving[0][:, n_word : n_word + n_words].bitcast(FP8X4),
                rhs_scale=moving[1][:, n_word : n_word + n_words],
                start=start,
                stop=stop,
            )

        e_raw = {}
        s_raw = {}
        w_raw = {}
        e_grouped = {}
        w_grouped = {}
        s_grouped = {}
        v_grouped = {}
        e_mx = {}
        w_mx = {}
        s_mx = {}
        v_mx = {}
        for part in PARTS:
            e_raw[part] = keep.tile([P, C_TILES, T], BF16, name="e_raw_" + part)
            s_raw[part] = keep.tile([P, PACK, T], BF16, name="s_raw_" + part)
            w_raw[part] = keep.tile([P, O_TILES, D2], BF16, name="w_raw_" + part)
            e_grouped[part] = keep.tile(
                [P, D2 * PACK], BF16, name="e_grouped_" + part, align_bytes=64
            )
            v_grouped[part] = keep.tile(
                [P, C_PASSES * T * PACK], BF16, name="v_grouped_" + part, align_bytes=64
            )
            e_mx[part] = mx_operand("e_" + part, D2)
            v_mx[part] = mx_operand("v_" + part, C_PASSES * T)
        for part in PARTS + ("neg_im",):
            s_grouped[part] = keep.tile(
                [P, T * PACK], BF16, name="s_grouped_" + part, align_bytes=64
            )
            s_mx[part] = mx_operand("s_" + part, T)
        for part in PARTS:
            w_grouped[part] = keep.tile(
                [P, C_PASSES * DIM * PACK], BF16, name="w_grouped_" + part, align_bytes=64
            )
            w_mx[part] = mx_operand("w_" + part, C_PASSES * DIM)

        e_dram = {"re": E_re, "im": E_im}
        s_dram = {"re": S_re, "im": S_im}
        w_dram = {"re": WPV_re, "im": WPV_im}

        def load_scores(u, half):
            cols = slice(half * HALF, (half + 1) * HALF)
            for part in PARTS:
                rows = s_dram[part].rearrange("b (u p e) j -> p (b u) e j", u=2, p=P, e=2)
                nc.sync.dma_start(
                    out=s_raw[part][:, 2 * u : 2 * u + 2, cols], in_=rows[:, u, :, cols]
                )

        def load_sequence(g):
            for part in PARTS:
                rows = e_dram[part].rearrange(
                    "b (a p e) i -> p (b a) (e i)", a=2 * C_PASSES, p=P, e=2
                )
                tiles = e_raw[part][:].rearrange("p (a e) i -> p a (e i)", e=2)
                nc.sync.dma_start(
                    out=tiles[:, 2 * g : 2 * g + 2, :], in_=rows[:, 2 * g : 2 * g + 2, :]
                )

        zeros = keep.tile([P, T], BF16, name="zeros")
        nc.vector.memset(zeros[:].bitcast(I32), 0)

        for part in PARTS:
            nc.vector.memset(s_raw[part][:, 2:4, 0:HALF], 0.0)
        load_scores(0, 0)
        load_sequence(0)
        load_sequence(1)
        load_scores(0, 1)
        load_scores(1, 1)
        for part in PARTS:
            nc.sync.dma_start(
                out=w_raw[part][:].rearrange("m x c -> m (x c)"),
                in_=w_dram[part].rearrange("(m x) c -> m (x c)", x=O_TILES),
            )

        def keep_warm(count):
            bank = banks.tile([P, T], F32, tag="bank")
            for n in range(count):
                nc.tensor.matmul(
                    out=bank[:], lhsT=zeros[:, 0:P], rhs=zeros[:], start=True, stop=True
                )

        column = keep.tile([P, T // P], I32, name="column")
        nc.gpsimd.iota(column[:], pattern=[[P, T // P]], base=0, channel_multiplier=1)
        inv_rho_column = keep.tile([P, T // P], F32, name="inv_rho_column")
        nc.vector.tensor_scalar(
            out=inv_rho_column[:], in0=column[:], scalar1=1.0, scalar2=None, op0=ALU.max
        )
        nc.vector.reciprocal(out=inv_rho_column[:], in_=inv_rho_column[:])
        ident = keep.tile([P, P], F32, name="ident")
        make_identity(nc, ident[:])
        keep_warm(2)
        spread = banks.tile([P, T // P, P], F32, tag="bank")
        for n in range(T // P):
            nc.tensor.matmul(
                out=spread[:, n, :],
                lhsT=inv_rho_column[:, n : n + 1].to_broadcast([P, P]),
                rhs=ident[:],
                start=True,
                stop=True,
            )
        keep_warm(2)
        inv_rho = keep.tile([P, T], F32, name="inv_rho")
        nc.scalar.copy(out=inv_rho[:], in_=spread[:].rearrange("m n p -> m (n p)"))
        distance = keep.tile([P, 2, HALF], I32, name="distance")
        nc.gpsimd.iota(distance[:], pattern=[[-1, 2], [1, HALF]], base=0, channel_multiplier=-2)
        keep_mask = keep.tile([P, 2, HALF], BF16, name="keep_mask")
        nc.vector.tensor_scalar(
            out=keep_mask[:], in0=distance[:], scalar1=0.0, scalar2=None, op0=ALU.is_ge
        )

        def prepare_scores(half):
            cols = slice(half * HALF, (half + 1) * HALF)
            for part in PARTS:
                square = s_raw[part][:, 2 * half : 2 * half + 2, cols]
                nc.vector.tensor_tensor(out=square, in0=square, in1=keep_mask[:], op=ALU.mult)
            for part in PARTS:
                nc.vector.tensor_copy(
                    out=s_grouped[part][:]
                    .rearrange("p (j t) -> p j t", t=PACK)[:, cols, :]
                    .rearrange("p (c r) t -> p c t r", r=4),
                    in_=s_raw[part][:, :, cols].rearrange("p t (c r) -> p c t r", r=4),
                )
            quantise(s_grouped["re"], s_mx["re"], half * HALF, HALF)
            values = slice(PACK * half * HALF, PACK * (half + 1) * HALF)
            nc.vector.tensor_scalar_mul(
                out=s_grouped["neg_im"][:, values], in0=s_grouped["im"][:, values], scalar1=-1.0
            )
            quantise(s_grouped["im"], s_mx["im"], half * HALF, HALF)
            quantise(s_grouped["neg_im"], s_mx["neg_im"], half * HALF, HALF)

        def transpose_words(bank, two_blocks, grouped_words, on_vector):
            for x in range(2):
                for u in range(2):
                    nc.tensor.transpose(
                        bank[:, x, u, :], two_blocks[x][:, u * P : (u + 1) * P], ident[:]
                    )
            if on_vector:
                nc.vector.tensor_copy(
                    out=grouped_words, in_=bank[:].rearrange("p x u m -> p x m u")
                )
            else:
                nc.scalar.copy(out=grouped_words, in_=bank[:].rearrange("p x u m -> p x m u"))

        def transpose_sequence(g):
            for part in PARTS:
                if (g, part) != (0, "re"):
                    keep_warm(1)
                words = e_grouped[part][:].bitcast(F32).rearrange(
                    "p (c m u) -> p c m u", c=C_TILES, m=P, u=2
                )
                for c in range(PACK * g, PACK * (g + 1), 2):
                    bank = banks.tile([P, 2, 2, P], F32, tag="bank")
                    transpose_words(
                        bank,
                        [e_raw[part][:, c + x, :].bitcast(F32) for x in range(2)],
                        words[:, c : c + 2, :, :],
                        on_vector=False,
                    )
            for part in PARTS:
                quantise(e_grouped[part], e_mx[part], g * K_PASS, K_PASS)

        def weight_word(pair, g, x):
            return ((pair * C_PASSES + g) * 2 + x) * P

        def transpose_weights(part):
            words = w_grouped[part][:].bitcast(F32).rearrange(
                "p (b x m u) -> p b x m u", b=O_PAIRS * C_PASSES, x=2, m=P, u=2
            )
            for pair in range(O_PAIRS):
                for g in range(C_PASSES):
                    pass_words = slice(g * K_PASS // 2, (g + 1) * K_PASS // 2)
                    bank = banks.tile([P, 2, 2, P], F32, tag="bank")
                    transpose_words(
                        bank,
                        [
                            w_raw[part][:, 2 * pair + x, :].bitcast(F32)[:, pass_words]
                            for x in range(2)
                        ],
                        words[:, pair * C_PASSES + g, :, :, :],
                        on_vector=(g == 1),
                    )
                first = weight_word(pair, 0, 0)
                count = C_PASSES * 2 * P
                quantise(w_grouped[part], w_mx[part], first, count)

        def first_stage(half, g):
            for part in PARTS:
                grouped = v_grouped[part][:].rearrange(
                    "p (g j t) -> p g j t", g=C_PASSES, j=T, t=PACK
                )
                for jt in range(half * J_TILES_PER_HALF, (half + 1) * J_TILES_PER_HALF):
                    bank = banks.tile([P, PACK, J_TILE], F32, tag="bank")
                    for t in range(PACK):
                        for n, (e_part, s_part) in enumerate(V_TERMS[part]):
                            mx_pass(
                                bank[:, t, :],
                                e_mx[e_part],
                                (PACK * g + t) * P,
                                s_mx[s_part],
                                jt * J_TILE,
                                J_TILE,
                                start=(n == 0),
                                stop=(n == 1),
                            )
                    nc.scalar.copy(
                        out=grouped[:, g, jt * J_TILE : (jt + 1) * J_TILE, :],
                        in_=bank[:].rearrange("p t j -> p j t"),
                    )
                quantise(v_grouped[part], v_mx[part], g * T + half * HALF, HALF)

        def second_stage(half):
            cols = slice(half * HALF, (half + 1) * HALF)
            out_dram = {"re": out_0, "im": out_1}
            def add_up(acc, pair, x, terms):
                passes = [(g, w, v) for g in range(C_PASSES) for (w, v) in terms]
                for n, (g, w_part, v_part) in enumerate(passes):
                    mx_pass(
                        acc,
                        w_mx[w_part],
                        weight_word(pair, g, x),
                        v_mx[v_part],
                        g * T + half * HALF,
                        HALF,
                        start=(n == 0),
                        stop=(n == len(passes) - 1),
                    )

            def store(part, pair, x, scaled):
                rows = out_dram[part].rearrange("b (m x) j -> m (b x) j", x=O_TILES)
                nc.sync.dma_start(out=rows[:, 2 * pair + x, cols], in_=scaled[:])

            for pair in range(O_PAIRS):
                for x in range(2):
                    minuend_term, subtrahend_term = OUT_TERMS["re"]
                    bank = banks.tile([P, HALF], F32, tag="bank")
                    add_up(bank[:], pair, x, [subtrahend_term])
                    minuend = banks.tile([P, HALF], F32, tag="bank")
                    add_up(minuend[:], pair, x, [minuend_term])
                    acc = banks.tile([P, HALF], F32, tag="bank")
                    add_up(acc[:], pair, x, OUT_TERMS["im"])
                    subtrahend = stores.tile([P, HALF], F32, tag="subtrahend")
                    nc.scalar.copy(out=subtrahend[:], in_=bank[:])
                    difference = stores.tile([P, HALF], F32, tag="difference")
                    nc.vector.tensor_tensor(
                        out=difference[:], in0=minuend[:], in1=subtrahend[:], op=ALU.subtract
                    )
                    scaled_im = stores.tile([P, HALF], F32, tag="scaled")
                    nc.vector.tensor_tensor(
                        out=scaled_im[:], in0=acc[:], in1=inv_rho[:, cols], op=ALU.mult
                    )
                    scaled_re = stores.tile([P, HALF], F32, tag="scaled")
                    nc.vector.tensor_tensor(
                        out=scaled_re[:], in0=difference[:], in1=inv_rho[:, cols], op=ALU.mult
                    )
                    store("im", pair, x, scaled_im)
                    store("re", pair, x, scaled_re)

        prepare_scores(0)
        transpose_sequence(0)
        transpose_sequence(1)
        prepare_scores(1)
        first_stage(0, 0)
        first_stage(0, 1)
        transpose_weights("re")
        first_stage(1, 0)
        transpose_weights("im")
        first_stage(1, 1)
        second_stage(0)
        second_stage(1)
